import numpy as np
import ml_dtypes


def mxq(x, axis, fmt="e4m3"):
    dtype, down = {"e4m3": (ml_dtypes.float8_e4m3fn, 7), "e5m2": (ml_dtypes.float8_e5m2, 14)}[fmt]
    v = np.moveaxis(np.asarray(x, np.float32).astype(ml_dtypes.bfloat16).astype(np.float64), axis, -1)
    blocks = v.reshape(v.shape[:-1] + (-1, 32))
    amax = np.abs(blocks).max(-1, keepdims=True)
    byte = np.maximum(np.where(amax > 0, np.frexp(amax)[1] - 1 + 127, 0) - down, 1)
    scale = np.exp2(byte - 127.0)
    codes = (blocks / scale).astype(np.float32).astype(dtype).astype(np.float64)
    return np.moveaxis((codes * scale).reshape(v.shape), -1, axis)


WIDE = False


def mx_kscale(k):
    if not WIDE:
        return np.ones(k)
    levels = np.array([30, -30])
    if k % 512:
        return np.exp2(np.random.permutation(np.resize(levels, k // 32))).repeat(32)
    a = np.empty((k // 512, 16))
    for p in range(k // 512):
        a[p, :8] = np.random.permutation(np.resize(levels, 8))
        for g in range(8):
            far = levels[np.abs(levels - a[p, g]) >= 10]
            a[p, g + 8] = far[np.random.randint(len(far))]
    return np.exp2(a.ravel()).repeat(32)


BF16 = ml_dtypes.bfloat16


def bf(x):
    return np.asarray(x, np.float32).astype(BF16)


def f64(x):
    return np.asarray(x).astype(np.float64)


I, H, B = 2048, 2048, 128


def sigmoid(v):
    return 1.0 / (1.0 + np.exp(-v))


def setup_inputs():
    s, t = mx_kscale(I), mx_kscale(H)
    d = {"x": bf(np.random.standard_normal((I, B)) * s[:, None]), "h": bf(np.random.standard_normal((B, H)) * t[None, :])}
    for n in ("w_ii", "w_ig"):
        d[n] = bf(np.random.standard_normal((H, I)) * 0.7 / np.sqrt(I) / s[None, :])
    for n in ("w_hi", "w_hg"):
        d[n] = bf(np.random.standard_normal((H, H)) * 0.7 / np.sqrt(H) / t[None, :])
    for n in ("b_ii", "b_hi", "b_ig", "b_hg"):
        d[n] = bf(np.random.standard_normal((H, 1)) * 0.3)
    return d


def reference(x, h, w_ii, w_ig, w_hi, w_hg, b_ii, b_hi, b_ig, b_hg):
    xq = mxq(f64(x), 0, "e4m3")
    hq = mxq(f64(h).T, 0, "e4m3")
    i = sigmoid((mxq(f64(w_ii), 1, "e5m2") @ xq) + f64(b_ii) + (mxq(f64(w_hi), 1, "e5m2") @ hq) + f64(b_hi))
    g = np.tanh((mxq(f64(w_ig), 1, "e5m2") @ xq) + f64(b_ig) + (mxq(f64(w_hg), 1, "e5m2") @ hq) + f64(b_hg))
    return i * g

@@ -1,0 +1,244 @@
+from contextlib import ExitStack
+
+import concourse.mybir as mybir
+from concourse.masks import make_identity
+
+F32 = mybir.dt.float32
+BF16 = mybir.dt.bfloat16
+U32 = mybir.dt.uint32
+U8 = mybir.dt.uint8
+E4 = mybir.dt.float8_e4m3fn_x4
+E5 = mybir.dt.float8_e5m2_x4
+ACT = mybir.ActivationFunctionType
+ALU = mybir.AluOpType
+
+P = 128
+K = 2048
+B = 128
+NSTEP = 32
+RAW_BUFS = 8
+LEAD = RAW_BUFS - 1
+
+FLOPS = 2 * 4 * 2048 * 2048 * 128
+
+
+def precopied(s, jj):
+    return jj == 0 and s > 0
+
+
+def vector_copies(s, g):
+    return g == 3 and s % 3 == 0
+
+
+def tile_naivelstm_pa_kernel(tc, x, h, w_ii, w_ig, w_hi, w_hg, b_ii, b_hi, b_ig, b_hg, out):
+    nc = tc.nc
+    weights = (w_ii, w_hi, w_ig, w_hg)
+
+    with ExitStack() as ctx:
+        const = ctx.enter_context(tc.tile_pool(name="const", bufs=1))
+        rawp = ctx.enter_context(tc.tile_pool(name="rawp", bufs=RAW_BUFS))
+        rawdp = ctx.enter_context(tc.tile_pool(name="rawdp", bufs=4))
+        grpp = ctx.enter_context(tc.tile_pool(name="grpp", bufs=8))
+        codep = ctx.enter_context(tc.tile_pool(name="codep", bufs=8))
+        epip = ctx.enter_context(tc.tile_pool(name="epip", bufs=2))
+        tpp = ctx.enter_context(tc.psum_pool(name="tpp", bufs=6))
+        accp = ctx.enter_context(tc.psum_pool(name="accp", bufs=2))
+        ctx.enter_context(tc.manual_schedule())
+
+        raw = {}
+        rawd = {}
+        grp = {}
+        codes = {}
+        acc = {}
+        acts = {}
+
+        def load(s):
+            u_idx, jp = divmod(s, 2)
+            n, mat = divmod(u_idx, 4)
+            t = rawp.tile([P, 2, K], BF16, name="raw", tag="raw")
+            src = weights[mat][512 * n : 512 * (n + 1), :].rearrange("(p j) k -> p j k", j=4)
+            src = src[:, 2 * jp : 2 * jp + 2, :]
+            if s == 0:
+                nc.sync.dma_start(out=t[:, :, 0:1024], in_=src[:, :, 0:1024])
+                nc.sync.dma_start(out=t[:, :, 1024:2048], in_=src[:, :, 1024:2048])
+            else:
+                nc.sync.dma_start(out=t[:], in_=src)
+            raw[s] = t
+
+        def precopy(s):
+            for jj in range(2):
+                if precopied(s, jj):
+                    d = rawdp.tile([P, 4, 2, 128], F32, name="rawd", tag="rawd")
+                    nc.vector.tensor_copy(
+                        out=d[:],
+                        in_=raw[s][:, jj, :].bitcast(F32).rearrange("p (g m u) -> p g u m", g=4, u=2),
+                    )
+                    rawd[(s, jj)] = d
+
+        def evacuate(eng_is_vector, dst, bank):
+            src = bank[:].rearrange("p u c -> p c u")
+            if eng_is_vector:
+                nc.vector.tensor_copy(out=dst, in_=src)
+            else:
+                nc.scalar.copy(out=dst, in_=src)
+
+        def quantize(u_idx, g):
+            wc = codep.tile([P, 512], U32, name="wc", tag="wc", align_bytes=64)
+            ws = codep.tile([P, 512], U8, name="ws", tag="ws", align_bytes=64)
+            nc.vector.quantize_mx(out=wc[:].bitcast(E5), scales=ws[:], in_=grp[(u_idx, g)][:])
+            codes[(u_idx, g)] = (wc, ws)
+
+        def multiply(u_idx, g):
+            n, mat = divmod(u_idx, 4)
+            gate = mat // 2
+            idx = (mat % 2) * 4 + g
+            if idx == 0:
+                acc[(n, gate)] = accp.tile([P, 512], F32, name="acc", tag="acc")
+            ac, asc = (xc, xs) if mat % 2 == 0 else (hc, hs)
+            wc, ws = codes[(u_idx, g)]
+            cols = slice(128 * g, 128 * (g + 1))
+            nc.tensor.matmul_mx(
+                out=acc[(n, gate)][:],
+                lhsT=ac[:, cols].bitcast(E4),
+                lhsT_scale=asc[:, cols],
+                rhs=wc[:].bitcast(E5),
+                rhs_scale=ws[:],
+                start=(idx == 0),
+                stop=(idx == 7),
+            )
+            return idx == 7
+
+        def epi_copy(n, gate):
+            zs = epip.tile([P, 512], F32, name="zs", tag="zs")
+            nc.vector.tensor_copy(out=zs[:], in_=acc[(n, gate)][:])
+            return zs
+
+        def epi_act(n, gate, zs):
+            zt = tpp.tile([P, 4, 128], F32, name="zt", tag="tp")
+            for j in range(4):
+                nc.tensor.transpose(zt[:, j, :], zs[:, 128 * j : 128 * (j + 1)], ident[:])
+            a = epip.tile([P, 4, 128], F32, name="act%d" % gate, tag="act%d" % gate)
+            func = ACT.Sigmoid if gate == 0 else ACT.Tanh
+            for j in range(4):
+                col = 4 * n + j
+                nc.scalar.activation(
+                    out=a[:, j, :], in_=zt[:, j, :], func=func, bias=bias[:, gate, col : col + 1], scale=1.0
+                )
+            acts[(n, gate)] = a
+
+        def epi_store(n):
+            ot = epip.tile([P, 4, 128], F32, name="ot", tag="ot")
+            nc.vector.tensor_tensor(out=ot[:], in0=acts[(n, 0)][:], in1=acts[(n, 1)][:], op=ALU.mult)
+            nc.sync.dma_start(
+                out=out[512 * n : 512 * (n + 1), :].rearrange("(p j) b -> p j b", j=4), in_=ot[:]
+            )
+
+        braw = const.tile([P, 4, 16], BF16, name="braw")
+        with nc.allow_non_contiguous_dma(reason="bias: 8-byte runs, once"):
+            for i, bvec in enumerate((b_ii, b_hi, b_ig, b_hg)):
+                nc.scalar.dma_start(
+                    out=braw[:, i, :].rearrange("p (n j) -> p n j", j=4),
+                    in_=bvec.rearrange("(n p j) o -> p n (j o)", p=P, j=4),
+                )
+        warm = const.tile([P, 1], F32, name="warm")
+        warm2 = const.tile([P, 1], F32, name="warm2")
+        nc.vector.memset(warm[:], 0.0)
+        nc.scalar.activation(out=warm2[:], in_=warm[:], func=ACT.Sigmoid)
+        ident = const.tile([P, P], F32, name="ident")
+        make_identity(nc, ident[:])
+
+        xraw = const.tile([P, 4, 512], BF16, name="xraw")
+        xgrp = const.tile([P, 2048], BF16, name="xgrp", align_bytes=64)
+        xc = const.tile([P, 512], U32, name="xc", align_bytes=64)
+        xs = const.tile([P, 512], U8, name="xs", align_bytes=64)
+        hraw = const.tile([P, K], BF16, name="hraw")
+        hgrp = const.tile([P, 2048], BF16, name="hgrp", align_bytes=64)
+        hc = const.tile([P, 512], U32, name="hc", align_bytes=64)
+        hs = const.tile([P, 512], U8, name="hs", align_bytes=64)
+        bias = const.tile([P, 2, 16], F32, name="bias")
+
+        load(0)
+        load(1)
+        nc.sync.dma_start(out=xraw[:], in_=x.rearrange("(g p j) b -> p g (j b)", p=P, j=4))
+        load(2)
+        nc.sync.dma_start(out=hraw[:], in_=h)
+        for s in range(3, LEAD):
+            load(s)
+
+        precopy(0)
+        pending = []
+
+        for s in range(NSTEP):
+            u_idx, jp = divmod(s, 2)
+            if s + LEAD < NSTEP:
+                load(s + LEAD)
+            if jp == 0 and u_idx > 0:
+                quantize(u_idx - 1, 3)
+            if s == 1:
+                nc.vector.tensor_copy(
+                    out=xgrp[:].rearrange("p (g b j) -> p g b j", g=4, j=4),
+                    in_=xraw[:].rearrange("p g (j b) -> p g b j", j=4),
+                )
+                nc.vector.quantize_mx(out=xc[:].bitcast(E4), scales=xs[:], in_=xgrp[:])
+            if s == 4:
+                for gate in range(2):
+                    nc.vector.tensor_tensor(
+                        out=bias[:, gate, :], in0=braw[:, 2 * gate, :], in1=braw[:, 2 * gate + 1, :], op=ALU.add
+                    )
+            if s + 1 < NSTEP:
+                precopy(s + 1)
+            if s == 3:
+                hw = hraw[:].bitcast(F32)
+                for gp in range(2):
+                    bank = tpp.tile([P, 2, 256], F32, name="hbank", tag="tp")
+                    for gg in range(2):
+                        g = 2 * gp + gg
+                        for u in range(2):
+                            nc.tensor.transpose(
+                                bank[:, u, 128 * gg : 128 * (gg + 1)], hw[:, 256 * g + u : 256 * (g + 1) : 2], ident[:]
+                            )
+                    dst = hgrp[:].bitcast(F32)[:, 512 * gp : 512 * (gp + 1)].rearrange("p (c u) -> p c u", u=2)
+                    evacuate(False, dst, bank)
+                nc.vector.quantize_mx(out=hc[:].bitcast(E4), scales=hs[:], in_=hgrp[:])
+
+            for g in range(4):
+                if jp == 0:
+                    grp[(u_idx, g)] = grpp.tile([P, 2048], BF16, name="grp", tag="grp", align_bytes=64)
+                bank = tpp.tile([P, 2, 256], F32, name="bank", tag="tp")
+                for jj in range(2):
+                    for u in range(2):
+                        if precopied(s, jj):
+                            src = rawd[(s, jj)][:, g, u, :]
+                        else:
+                            src = raw[s][:, jj, :].bitcast(F32)[:, 256 * g + u : 256 * (g + 1) : 2]
+                        nc.tensor.transpose(bank[:, u, 128 * jj : 128 * (jj + 1)], src, ident[:])
+                dst = grp[(u_idx, g)][:].bitcast(F32)[:, 512 * jp : 512 * (jp + 1)]
+                evacuate(vector_copies(s, g), dst.rearrange("p (c u) -> p c u", u=2), bank)
+                if jp == 1 and g >= 1:
+                    quantize(u_idx, g - 1)
+
+            still = []
+            for item in pending:
+                if item[0] == "act":
+                    epi_act(item[1], item[2], item[3])
+                    if item[2] == 1:
+                        still.append(("store", item[1]))
+                else:
+                    epi_store(item[1])
+            pending = still
+
+            if s >= 2:
+                mu = (s - 2) // 2
+                for g in (2 * (s % 2), 2 * (s % 2) + 1):
+                    if multiply(mu, g):
+                        n, mat = divmod(mu, 4)
+                        pending.append(("act", n, mat // 2, epi_copy(n, mat // 2)))
+
+        quantize(15, 3)
+        for item in pending:
+            epi_store(item[1])
+        for g in range(4):
+            multiply(15, g)
+        zs = epi_copy(3, 1)
+        epi_act(3, 1, zs)
+        epi_store(3)

@@ -23,11 +23,11 @@ FLOPS = 2 * 4 * 2048 * 2048 * 128
 
 
 def precopied(s, jj):
-    return jj == 0 and s > 0
+    return s > 0 and (jj == 0 or s % 2 == 1)
 
 
 def vector_copies(s, g):
-    return g == 3 and s % 3 == 0
+    return False
 
 
 def tile_naivelstm_pa_kernel(tc, x, h, w_ii, w_ig, w_hi, w_hg, b_ii, b_hi, b_ig, b_hg, out):
@@ -37,9 +37,9 @@ def tile_naivelstm_pa_kernel(tc, x, h, w_ii, w_ig, w_hi, w_hg, b_ii, b_hi, b_ig,
     with ExitStack() as ctx:
         const = ctx.enter_context(tc.tile_pool(name="const", bufs=1))
         rawp = ctx.enter_context(tc.tile_pool(name="rawp", bufs=RAW_BUFS))
-        rawdp = ctx.enter_context(tc.tile_pool(name="rawdp", bufs=4))
+        rawdp = ctx.enter_context(tc.tile_pool(name="rawdp", bufs=6))
         grpp = ctx.enter_context(tc.tile_pool(name="grpp", bufs=8))
-        codep = ctx.enter_context(tc.tile_pool(name="codep", bufs=8))
+        codep = ctx.enter_context(tc.tile_pool(name="codep", bufs=12))
         epip = ctx.enter_context(tc.tile_pool(name="epip", bufs=2))
         tpp = ctx.enter_context(tc.psum_pool(name="tpp", bufs=6))
         accp = ctx.enter_context(tc.psum_pool(name="accp", bufs=2))
@@ -59,8 +59,8 @@ def tile_naivelstm_pa_kernel(tc, x, h, w_ii, w_ig, w_hi, w_hg, b_ii, b_hi, b_ig,
             src = weights[mat][512 * n : 512 * (n + 1), :].rearrange("(p j) k -> p j k", j=4)
             src = src[:, 2 * jp : 2 * jp + 2, :]
             if s == 0:
-                nc.sync.dma_start(out=t[:, :, 0:1024], in_=src[:, :, 0:1024])
-                nc.sync.dma_start(out=t[:, :, 1024:2048], in_=src[:, :, 1024:2048])
+                for g in range(4):
+                    nc.sync.dma_start(out=t[:, :, 512 * g : 512 * (g + 1)], in_=src[:, :, 512 * g : 512 * (g + 1)])
             else:
                 nc.sync.dma_start(out=t[:], in_=src)
             raw[s] = t
@@ -166,6 +166,7 @@ def tile_naivelstm_pa_kernel(tc, x, h, w_ii, w_ig, w_hi, w_hg, b_ii, b_hi, b_ig,
             load(s)
 
         precopy(0)
+        precopy(1)
         pending = []
 
         for s in range(NSTEP):
@@ -174,7 +175,7 @@ def tile_naivelstm_pa_kernel(tc, x, h, w_ii, w_ig, w_hi, w_hg, b_ii, b_hi, b_ig,
                 load(s + LEAD)
             if jp == 0 and u_idx > 0:
                 quantize(u_idx - 1, 3)
-            if s == 1:
+            if s == 0:
                 nc.vector.tensor_copy(
                     out=xgrp[:].rearrange("p (g b j) -> p g b j", g=4, j=4),
                     in_=xraw[:].rearrange("p g (j b) -> p g b j", j=4),
@@ -185,8 +186,8 @@ def tile_naivelstm_pa_kernel(tc, x, h, w_ii, w_ig, w_hi, w_hg, b_ii, b_hi, b_ig,
                     nc.vector.tensor_tensor(
                         out=bias[:, gate, :], in0=braw[:, 2 * gate, :], in1=braw[:, 2 * gate + 1, :], op=ALU.add
                     )
-            if s + 1 < NSTEP:
-                precopy(s + 1)
+            if s + 2 < NSTEP:
+                precopy(s + 2)
             if s == 3:
                 hw = hraw[:].bitcast(F32)
                 for gp in range(2):
@@ -227,16 +228,16 @@ def tile_naivelstm_pa_kernel(tc, x, h, w_ii, w_ig, w_hi, w_hg, b_ii, b_hi, b_ig,
                     epi_store(item[1])
             pending = still
 
-            if s >= 2:
-                mu = (s - 2) // 2
-                for g in (2 * (s % 2), 2 * (s % 2) + 1):
+            if s >= 3:
+                mu, half = divmod(s - 3, 2)
+                for g in (2 * half, 2 * half + 1):
                     if multiply(mu, g):
                         n, mat = divmod(mu, 4)
                         pending.append(("act", n, mat // 2, epi_copy(n, mat // 2)))
 
         quantize(15, 3)
-        for item in pending:
-            epi_store(item[1])
+        multiply(14, 2)
+        multiply(14, 3)
         for g in range(4):
             multiply(15, g)
         zs = epi_copy(3, 1)

@@ -22,8 +22,11 @@ LEAD = RAW_BUFS - 1
 FLOPS = 2 * 4 * 2048 * 2048 * 128
 
 
-def precopied(s, jj):
-    return s > 0 and (jj == 0 or s % 2 == 1)
+NA = 6
+
+
+def precopied(s, jj, g):
+    return s > 0 and 4 * jj + g < NA
 
 
 def vector_copies(s, g):
@@ -37,7 +40,7 @@ def tile_naivelstm_pa_kernel(tc, x, h, w_ii, w_ig, w_hi, w_hg, b_ii, b_hi, b_ig,
     with ExitStack() as ctx:
         const = ctx.enter_context(tc.tile_pool(name="const", bufs=1))
         rawp = ctx.enter_context(tc.tile_pool(name="rawp", bufs=RAW_BUFS))
-        rawdp = ctx.enter_context(tc.tile_pool(name="rawdp", bufs=6))
+        rawdp = ctx.enter_context(tc.tile_pool(name="rawdp", bufs=4))
         grpp = ctx.enter_context(tc.tile_pool(name="grpp", bufs=8))
         codep = ctx.enter_context(tc.tile_pool(name="codep", bufs=12))
         epip = ctx.enter_context(tc.tile_pool(name="epip", bufs=2))
@@ -66,14 +69,13 @@ def tile_naivelstm_pa_kernel(tc, x, h, w_ii, w_ig, w_hi, w_hg, b_ii, b_hi, b_ig,
             raw[s] = t
 
         def precopy(s):
-            for jj in range(2):
-                if precopied(s, jj):
-                    d = rawdp.tile([P, 4, 2, 128], F32, name="rawd", tag="rawd")
-                    nc.vector.tensor_copy(
-                        out=d[:],
-                        in_=raw[s][:, jj, :].bitcast(F32).rearrange("p (g m u) -> p g u m", g=4, u=2),
-                    )
-                    rawd[(s, jj)] = d
+            if s > 0:
+                d = rawdp.tile([P, 2, NA, 128], F32, name="rawd", tag="rawd")
+                words = raw[s][:].rearrange("p j k -> p (j k)").bitcast(F32)
+                nc.vector.tensor_copy(
+                    out=d[:], in_=words[:, 0 : 256 * NA].rearrange("p (a m u) -> p u a m", a=NA, u=2)
+                )
+                rawd[s] = d
 
         def evacuate(eng_is_vector, dst, bank):
             src = bank[:].rearrange("p u c -> p c u")
@@ -208,8 +210,8 @@ def tile_naivelstm_pa_kernel(tc, x, h, w_ii, w_ig, w_hi, w_hg, b_ii, b_hi, b_ig,
                 bank = tpp.tile([P, 2, 256], F32, name="bank", tag="tp")
                 for jj in range(2):
                     for u in range(2):
-                        if precopied(s, jj):
-                            src = rawd[(s, jj)][:, g, u, :]
+                        if precopied(s, jj, g):
+                            src = rawd[s][:, u, 4 * jj + g, :]
                         else:
                             src = raw[s][:, jj, :].bitcast(F32)[:, 256 * g + u : 256 * (g + 1) : 2]
                         nc.tensor.transpose(bank[:, u, 128 * jj : 128 * (jj + 1)], src, ident[:])
@@ -228,18 +230,29 @@ def tile_naivelstm_pa_kernel(tc, x, h, w_ii, w_ig, w_hi, w_hg, b_ii, b_hi, b_ig,
                     epi_store(item[1])
             pending = still
 
-            if s >= 3:
-                mu, half = divmod(s - 3, 2)
-                for g in (2 * half, 2 * half + 1):
+            if s >= 4 and s % 2 == 0:
+                mu = (s - 4) // 2
+                for g in range(4):
                     if multiply(mu, g):
                         n, mat = divmod(mu, 4)
                         pending.append(("act", n, mat // 2, epi_copy(n, mat // 2)))
 
         quantize(15, 3)
-        multiply(14, 2)
-        multiply(14, 3)
+        for g in range(4):
+            multiply(14, g)
         for g in range(4):
             multiply(15, g)
-        zs = epi_copy(3, 1)
-        epi_act(3, 1, zs)
-        epi_store(3)
+        zs = epip.tile([P, 512], F32, name="zs", tag="zs")
+        ga = epip.tile([P, 4, 128], F32, name="act1", tag="act1")
+        ot = epip.tile([P, 4, 128], F32, name="ot", tag="ot")
+        for j in range(4):
+            nc.vector.tensor_copy(out=zs[:, 128 * j : 128 * (j + 1)], in_=acc[(3, 1)][:, 128 * j : 128 * (j + 1)])
+        for j in range(4):
+            zt = tpp.tile([P, 4, 128], F32, name="zt", tag="tp")
+            nc.tensor.transpose(zt[:, 0, :], zs[:, 128 * j : 128 * (j + 1)], ident[:])
+            nc.scalar.activation(
+                out=ga[:, j, :], in_=zt[:, 0, :], func=ACT.Tanh, bias=bias[:, 1, 12 + j : 13 + j], scale=1.0
+            )
+        for j in range(4):
+            nc.vector.tensor_tensor(out=ot[:, j, :], in0=acts[(3, 0)][:, j, :], in1=ga[:, j, :], op=ALU.mult)
+        nc.sync.dma_start(out=out[1536:2048, :].rearrange("(p j) b -> p j b", j=4), in_=ot[:])

@@ -22,7 +22,7 @@ LEAD = RAW_BUFS - 1
 FLOPS = 2 * 4 * 2048 * 2048 * 128
 
 
-NA = 6
+NA = 4
 
 
 def precopied(s, jj, g):
@@ -30,7 +30,7 @@ def precopied(s, jj, g):
 
 
 def vector_copies(s, g):
-    return False
+    return s % 4 == 2 and g == 2
 
 
 def tile_naivelstm_pa_kernel(tc, x, h, w_ii, w_ig, w_hi, w_hg, b_ii, b_hi, b_ig, b_hg, out):

@@ -25,12 +25,15 @@ FLOPS = 2 * 4 * 2048 * 2048 * 128
 NA = 4
 
 
+FIRST_Q = 6
+
+
 def precopied(s, jj, g):
-    return s > 0 and 4 * jj + g < NA
+    return s >= FIRST_Q and 4 * jj + g < NA
 
 
 def vector_copies(s, g):
-    return s % 4 == 2 and g == 2
+    return s >= FIRST_Q and s % 2 == 0 and g == 2
 
 
 def tile_naivelstm_pa_kernel(tc, x, h, w_ii, w_ig, w_hi, w_hg, b_ii, b_hi, b_ig, b_hg, out):
@@ -44,8 +47,8 @@ def tile_naivelstm_pa_kernel(tc, x, h, w_ii, w_ig, w_hi, w_hg, b_ii, b_hi, b_ig,
         grpp = ctx.enter_context(tc.tile_pool(name="grpp", bufs=8))
         codep = ctx.enter_context(tc.tile_pool(name="codep", bufs=12))
         epip = ctx.enter_context(tc.tile_pool(name="epip", bufs=2))
-        tpp = ctx.enter_context(tc.psum_pool(name="tpp", bufs=6))
-        accp = ctx.enter_context(tc.psum_pool(name="accp", bufs=2))
+        tpp = ctx.enter_context(tc.psum_pool(name="tpp", bufs=7))
+        accp = ctx.enter_context(tc.psum_pool(name="accp", bufs=1))
         ctx.enter_context(tc.manual_schedule())
 
         raw = {}
@@ -69,7 +72,7 @@ def tile_naivelstm_pa_kernel(tc, x, h, w_ii, w_ig, w_hi, w_hg, b_ii, b_hi, b_ig,
             raw[s] = t
 
         def precopy(s):
-            if s > 0:
+            if s >= FIRST_Q:
                 d = rawdp.tile([P, 2, NA, 128], F32, name="rawd", tag="rawd")
                 words = raw[s][:].rearrange("p j k -> p (j k)").bitcast(F32)
                 nc.vector.tensor_copy(
@@ -222,12 +225,14 @@ def tile_naivelstm_pa_kernel(tc, x, h, w_ii, w_ig, w_hi, w_hg, b_ii, b_hi, b_ig,
 
             still = []
             for item in pending:
-                if item[0] == "act":
-                    epi_act(item[1], item[2], item[3])
-                    if item[2] == 1:
-                        still.append(("store", item[1]))
+                if item[0] > s:
+                    still.append(item)
+                elif item[1] == "act":
+                    epi_act(item[2], item[3], item[4])
+                    if item[3] == 1:
+                        still.append((s + 1, "store", item[2]))
                 else:
-                    epi_store(item[1])
+                    epi_store(item[2])
             pending = still
 
             if s >= 4 and s % 2 == 0:
@@ -235,8 +240,10 @@ def tile_naivelstm_pa_kernel(tc, x, h, w_ii, w_ig, w_hi, w_hg, b_ii, b_hi, b_ig,
                 for g in range(4):
                     if multiply(mu, g):
                         n, mat = divmod(mu, 4)
-                        pending.append(("act", n, mat // 2, epi_copy(n, mat // 2)))
+                        pending.append((s + 2, "act", n, mat // 2, epi_copy(n, mat // 2)))
 
+        for item in pending:
+            epi_act(item[2], item[3], item[4])
         quantize(15, 3)
         for g in range(4):
             multiply(14, g)

@@ -47,6 +47,7 @@ def tile_naivelstm_pa_kernel(tc, x, h, w_ii, w_ig, w_hi, w_hg, b_ii, b_hi, b_ig,
         grpp = ctx.enter_context(tc.tile_pool(name="grpp", bufs=8))
         codep = ctx.enter_context(tc.tile_pool(name="codep", bufs=12))
         epip = ctx.enter_context(tc.tile_pool(name="epip", bufs=2))
+        outp = ctx.enter_context(tc.tile_pool(name="outp", bufs=4))
         tpp = ctx.enter_context(tc.psum_pool(name="tpp", bufs=7))
         accp = ctx.enter_context(tc.psum_pool(name="accp", bufs=1))
         ctx.enter_context(tc.manual_schedule())
@@ -57,13 +58,13 @@ def tile_naivelstm_pa_kernel(tc, x, h, w_ii, w_ig, w_hi, w_hg, b_ii, b_hi, b_ig,
         codes = {}
         acc = {}
         acts = {}
+        to_store = []
 
         def load(s):
             u_idx, jp = divmod(s, 2)
             n, mat = divmod(u_idx, 4)
             t = rawp.tile([P, 2, K], BF16, name="raw", tag="raw")
-            src = weights[mat][512 * n : 512 * (n + 1), :].rearrange("(p j) k -> p j k", j=4)
-            src = src[:, 2 * jp : 2 * jp + 2, :]
+            src = weights[mat].rearrange("(p n j) k -> p n j k", n=4, j=4)[:, n, 2 * jp : 2 * jp + 2, :]
             if s == 0:
                 for g in range(4):
                     nc.sync.dma_start(out=t[:, :, 512 * g : 512 * (g + 1)], in_=src[:, :, 512 * g : 512 * (g + 1)])
@@ -132,19 +133,16 @@ def tile_naivelstm_pa_kernel(tc, x, h, w_ii, w_ig, w_hi, w_hg, b_ii, b_hi, b_ig,
             acts[(n, gate)] = a
 
         def epi_store(n):
-            ot = epip.tile([P, 4, 128], F32, name="ot", tag="ot")
+            ot = outp.tile([P, 4, 128], F32, name="ot", tag="ot")
             nc.vector.tensor_tensor(out=ot[:], in0=acts[(n, 0)][:], in1=acts[(n, 1)][:], op=ALU.mult)
-            nc.sync.dma_start(
-                out=out[512 * n : 512 * (n + 1), :].rearrange("(p j) b -> p j b", j=4), in_=ot[:]
-            )
+            to_store.append((n, ot))
+
+        def store_ready():
+            for n, ot in to_store:
+                nc.sync.dma_start(out=out.rearrange("(p n j) b -> p n j b", n=4, j=4)[:, n, :, :], in_=ot[:])
+            to_store.clear()
 
         braw = const.tile([P, 4, 16], BF16, name="braw")
-        with nc.allow_non_contiguous_dma(reason="bias: 8-byte runs, once"):
-            for i, bvec in enumerate((b_ii, b_hi, b_ig, b_hg)):
-                nc.scalar.dma_start(
-                    out=braw[:, i, :].rearrange("p (n j) -> p n j", j=4),
-                    in_=bvec.rearrange("(n p j) o -> p n (j o)", p=P, j=4),
-                )
         warm = const.tile([P, 1], F32, name="warm")
         warm2 = const.tile([P, 1], F32, name="warm2")
         nc.vector.memset(warm[:], 0.0)
@@ -169,6 +167,8 @@ def tile_naivelstm_pa_kernel(tc, x, h, w_ii, w_ig, w_hi, w_hg, b_ii, b_hi, b_ig,
         nc.sync.dma_start(out=hraw[:], in_=h)
         for s in range(3, LEAD):
             load(s)
+        for i, bvec in enumerate((b_ii, b_hi, b_ig, b_hg)):
+            nc.sync.dma_start(out=braw[:, i, :], in_=bvec.rearrange("(p c) o -> p (c o)", c=16))
 
         precopy(0)
         precopy(1)
@@ -186,7 +186,7 @@ def tile_naivelstm_pa_kernel(tc, x, h, w_ii, w_ig, w_hi, w_hg, b_ii, b_hi, b_ig,
                     in_=xraw[:].rearrange("p g (j b) -> p g b j", j=4),
                 )
                 nc.vector.quantize_mx(out=xc[:].bitcast(E4), scales=xs[:], in_=xgrp[:])
-            if s == 4:
+            if s == 7:
                 for gate in range(2):
                     nc.vector.tensor_tensor(
                         out=bias[:, gate, :], in0=braw[:, 2 * gate, :], in1=braw[:, 2 * gate + 1, :], op=ALU.add
@@ -234,6 +234,8 @@ def tile_naivelstm_pa_kernel(tc, x, h, w_ii, w_ig, w_hi, w_hg, b_ii, b_hi, b_ig,
                 else:
                     epi_store(item[2])
             pending = still
+            if s + LEAD >= NSTEP - 1:
+                store_ready()
 
             if s >= 4 and s % 2 == 0:
                 mu = (s - 4) // 2
@@ -251,7 +253,7 @@ def tile_naivelstm_pa_kernel(tc, x, h, w_ii, w_ig, w_hi, w_hg, b_ii, b_hi, b_ig,
             multiply(15, g)
         zs = epip.tile([P, 512], F32, name="zs", tag="zs")
         ga = epip.tile([P, 4, 128], F32, name="act1", tag="act1")
-        ot = epip.tile([P, 4, 128], F32, name="ot", tag="ot")
+        ot = outp.tile([P, 4, 128], F32, name="ot", tag="ot")
         for j in range(4):
             nc.vector.tensor_copy(out=zs[:, 128 * j : 128 * (j + 1)], in_=acc[(3, 1)][:, 128 * j : 128 * (j + 1)])
         for j in range(4):
@@ -262,4 +264,4 @@ def tile_naivelstm_pa_kernel(tc, x, h, w_ii, w_ig, w_hi, w_hg, b_ii, b_hi, b_ig,
             )
         for j in range(4):
             nc.vector.tensor_tensor(out=ot[:, j, :], in0=acts[(3, 0)][:, j, :], in1=ga[:, j, :], op=ALU.mult)
-        nc.sync.dma_start(out=out[1536:2048, :].rearrange("(p j) b -> p j b", j=4), in_=ot[:])
+        nc.sync.dma_start(out=out.rearrange("(p n j) b -> p n j b", n=4, j=4)[:, 3, :, :], in_=ot[:])

@@ -14,42 +14,65 @@ ALU = mybir.AluOpType
 
 P = 128
 K = 2048
-B = 128
 NSTEP = 32
 RAW_BUFS = 8
 LEAD = RAW_BUFS - 1
 
 FLOPS = 2 * 4 * 2048 * 2048 * 128
 
-
-NA = 4
-
-
-FIRST_Q = 6
+NA = 5
+FIRST_Q = 5
+LAST_Q = 32
+MMU = 1
+MM_LAG = 2
+CODE_BUFS = 12
+X_AFTER = 1
+X_STEP = 0
+H_AFTER = 2
+H_STEP = 3
+ACT_LAG = 2
+TP_BUFS = 7
+ACC_BUFS = 1
+VE_MOD = 16
+VE_PH = 2
+XFIRST = 0
+LAST_PIECES = 0
+BIAS_AFTER = 6
+BIAS_STEP = 7
+PC_LEAD = 2
+DVE_ORDER = 1
+PC_POS = 0
 
 
 def precopied(s, jj, g):
-    return s >= FIRST_Q and 4 * jj + g < NA
+    return FIRST_Q <= s < LAST_Q and 4 * jj + g < NA
 
 
 def vector_copies(s, g):
-    return s >= FIRST_Q and s % 2 == 0 and g == 2
+    return s >= FIRST_Q and (4 * s + g) % VE_MOD == VE_PH
 
 
 def tile_naivelstm_pa_kernel(tc, x, h, w_ii, w_ig, w_hi, w_hg, b_ii, b_hi, b_ig, b_hg, out):
     nc = tc.nc
-    weights = (w_ii, w_hi, w_ig, w_hg)
+    units = []
+    for n in range(4):
+        if n == 0 and XFIRST:
+            order = ((w_ii, 0, True), (w_ig, 1, True), (w_hi, 0, False), (w_hg, 1, False))
+        else:
+            order = ((w_ii, 0, True), (w_hi, 0, False), (w_ig, 1, True), (w_hg, 1, False))
+        for w, gate, from_x in order:
+            units.append((w, n, gate, from_x))
 
     with ExitStack() as ctx:
         const = ctx.enter_context(tc.tile_pool(name="const", bufs=1))
         rawp = ctx.enter_context(tc.tile_pool(name="rawp", bufs=RAW_BUFS))
         rawdp = ctx.enter_context(tc.tile_pool(name="rawdp", bufs=4))
         grpp = ctx.enter_context(tc.tile_pool(name="grpp", bufs=8))
-        codep = ctx.enter_context(tc.tile_pool(name="codep", bufs=12))
+        codep = ctx.enter_context(tc.tile_pool(name="codep", bufs=CODE_BUFS))
         epip = ctx.enter_context(tc.tile_pool(name="epip", bufs=2))
         outp = ctx.enter_context(tc.tile_pool(name="outp", bufs=4))
-        tpp = ctx.enter_context(tc.psum_pool(name="tpp", bufs=7))
-        accp = ctx.enter_context(tc.psum_pool(name="accp", bufs=1))
+        tpp = ctx.enter_context(tc.psum_pool(name="tpp", bufs=TP_BUFS))
+        accp = ctx.enter_context(tc.psum_pool(name="accp", bufs=ACC_BUFS))
         ctx.enter_context(tc.manual_schedule())
 
         raw = {}
@@ -62,10 +85,10 @@ def tile_naivelstm_pa_kernel(tc, x, h, w_ii, w_ig, w_hi, w_hg, b_ii, b_hi, b_ig,
 
         def load(s):
             u_idx, jp = divmod(s, 2)
-            n, mat = divmod(u_idx, 4)
+            w, n, gate, from_x = units[u_idx]
             t = rawp.tile([P, 2, K], BF16, name="raw", tag="raw")
-            src = weights[mat].rearrange("(p n j) k -> p n j k", n=4, j=4)[:, n, 2 * jp : 2 * jp + 2, :]
-            if s == 0:
+            src = w.rearrange("(p n j) k -> p n j k", n=4, j=4)[:, n, 2 * jp : 2 * jp + 2, :]
+            if s == 0 or (LAST_PIECES and s == NSTEP - 1):
                 for g in range(4):
                     nc.sync.dma_start(out=t[:, :, 512 * g : 512 * (g + 1)], in_=src[:, :, 512 * g : 512 * (g + 1)])
             else:
@@ -73,7 +96,7 @@ def tile_naivelstm_pa_kernel(tc, x, h, w_ii, w_ig, w_hi, w_hg, b_ii, b_hi, b_ig,
             raw[s] = t
 
         def precopy(s):
-            if s >= FIRST_Q:
+            if FIRST_Q <= s < LAST_Q:
                 d = rawdp.tile([P, 2, NA, 128], F32, name="rawd", tag="rawd")
                 words = raw[s][:].rearrange("p j k -> p (j k)").bitcast(F32)
                 nc.vector.tensor_copy(
@@ -95,12 +118,10 @@ def tile_naivelstm_pa_kernel(tc, x, h, w_ii, w_ig, w_hi, w_hg, b_ii, b_hi, b_ig,
             codes[(u_idx, g)] = (wc, ws)
 
         def multiply(u_idx, g):
-            n, mat = divmod(u_idx, 4)
-            gate = mat // 2
-            idx = (mat % 2) * 4 + g
-            if idx == 0:
+            w, n, gate, from_x = units[u_idx]
+            if from_x and g == 0:
                 acc[(n, gate)] = accp.tile([P, 512], F32, name="acc", tag="acc")
-            ac, asc = (xc, xs) if mat % 2 == 0 else (hc, hs)
+            ac, asc = (xc, xs) if from_x else (hc, hs)
             wc, ws = codes[(u_idx, g)]
             cols = slice(128 * g, 128 * (g + 1))
             nc.tensor.matmul_mx(
@@ -109,10 +130,10 @@ def tile_naivelstm_pa_kernel(tc, x, h, w_ii, w_ig, w_hi, w_hg, b_ii, b_hi, b_ig,
                 lhsT_scale=asc[:, cols],
                 rhs=wc[:].bitcast(E5),
                 rhs_scale=ws[:],
-                start=(idx == 0),
-                stop=(idx == 7),
+                start=(from_x and g == 0),
+                stop=(not from_x and g == 3),
             )
-            return idx == 7
+            return not from_x and g == 3
 
         def epi_copy(n, gate):
             zs = epip.tile([P, 512], F32, name="zs", tag="zs")
@@ -160,40 +181,44 @@ def tile_naivelstm_pa_kernel(tc, x, h, w_ii, w_ig, w_hi, w_hg, b_ii, b_hi, b_ig,
         hs = const.tile([P, 512], U8, name="hs", align_bytes=64)
         bias = const.tile([P, 2, 16], F32, name="bias")
 
-        load(0)
-        load(1)
-        nc.sync.dma_start(out=xraw[:], in_=x.rearrange("(g p j) b -> p g (j b)", p=P, j=4))
-        load(2)
-        nc.sync.dma_start(out=hraw[:], in_=h)
-        for s in range(3, LEAD):
+        def load_more(s):
             load(s)
-        for i, bvec in enumerate((b_ii, b_hi, b_ig, b_hg)):
-            nc.sync.dma_start(out=braw[:, i, :], in_=bvec.rearrange("(p c) o -> p (c o)", c=16))
+            if s == X_AFTER:
+                nc.sync.dma_start(out=xraw[:], in_=x.rearrange("(g p j) b -> p g (j b)", p=P, j=4))
+            if s == H_AFTER:
+                nc.sync.dma_start(out=hraw[:], in_=h)
+            if s == BIAS_AFTER:
+                for i, bvec in enumerate((b_ii, b_hi, b_ig, b_hg)):
+                    nc.sync.dma_start(out=braw[:, i, :], in_=bvec.rearrange("(p c) o -> p (c o)", c=16))
 
-        precopy(0)
-        precopy(1)
+        for s in range(LEAD):
+            load_more(s)
+
+        for s in range(PC_LEAD):
+            precopy(s)
         pending = []
+        mm_done = []
 
         for s in range(NSTEP):
             u_idx, jp = divmod(s, 2)
             if s + LEAD < NSTEP:
-                load(s + LEAD)
-            if jp == 0 and u_idx > 0:
+                load_more(s + LEAD)
+            if jp == 0 and u_idx > 0 and not DVE_ORDER:
                 quantize(u_idx - 1, 3)
-            if s == 0:
+            if s == X_STEP:
                 nc.vector.tensor_copy(
                     out=xgrp[:].rearrange("p (g b j) -> p g b j", g=4, j=4),
                     in_=xraw[:].rearrange("p g (j b) -> p g b j", j=4),
                 )
                 nc.vector.quantize_mx(out=xc[:].bitcast(E4), scales=xs[:], in_=xgrp[:])
-            if s == 7:
+            if s == BIAS_STEP:
                 for gate in range(2):
                     nc.vector.tensor_tensor(
                         out=bias[:, gate, :], in0=braw[:, 2 * gate, :], in1=braw[:, 2 * gate + 1, :], op=ALU.add
                     )
-            if s + 2 < NSTEP:
-                precopy(s + 2)
-            if s == 3:
+            if s + PC_LEAD < NSTEP and PC_POS == 0 and not DVE_ORDER:
+                precopy(s + PC_LEAD)
+            if s == H_STEP:
                 hw = hraw[:].bitcast(F32)
                 for gp in range(2):
                     bank = tpp.tile([P, 2, 256], F32, name="hbank", tag="tp")
@@ -220,8 +245,22 @@ def tile_naivelstm_pa_kernel(tc, x, h, w_ii, w_ig, w_hi, w_hg, b_ii, b_hi, b_ig,
                         nc.tensor.transpose(bank[:, u, 128 * jj : 128 * (jj + 1)], src, ident[:])
                 dst = grp[(u_idx, g)][:].bitcast(F32)[:, 512 * jp : 512 * (jp + 1)]
                 evacuate(vector_copies(s, g), dst.rearrange("p (c u) -> p c u", u=2), bank)
-                if jp == 1 and g >= 1:
+                if jp == 1 and g >= 1 and not DVE_ORDER:
                     quantize(u_idx, g - 1)
+                if s + PC_LEAD < NSTEP and PC_POS == g + 1 and not DVE_ORDER:
+                    precopy(s + PC_LEAD)
+                if DVE_ORDER:
+                    if jp == 1 and g in (1, 2):
+                        quantize(u_idx, g - 1)
+                    if jp == 1 and g == 3:
+                        if s + 2 < NSTEP:
+                            precopy(s + 2)
+                        quantize(u_idx, 2)
+                    if jp == 0 and g == 2:
+                        if u_idx > 0:
+                            quantize(u_idx - 1, 3)
+                        if s + 2 < NSTEP:
+                            precopy(s + 2)
 
             still = []
             for item in pending:
@@ -237,20 +276,21 @@ def tile_naivelstm_pa_kernel(tc, x, h, w_ii, w_ig, w_hi, w_hg, b_ii, b_hi, b_ig,
             if s + LEAD >= NSTEP - 1:
                 store_ready()
 
-            if s >= 4 and s % 2 == 0:
-                mu = (s - 4) // 2
-                for g in range(4):
-                    if multiply(mu, g):
-                        n, mat = divmod(mu, 4)
-                        pending.append((s + 2, "act", n, mat // 2, epi_copy(n, mat // 2)))
+            if (s - MM_LAG + 1) % (2 * MMU) == 0 and s > MM_LAG:
+                q = (s - MM_LAG + 1) // (2 * MMU) - 1
+                for mu in range(q * MMU, (q + 1) * MMU):
+                    mm_done.append(mu)
+                    for g in range(4):
+                        if multiply(mu, g):
+                            pending.append((s + ACT_LAG, "act", units[mu][1], units[mu][2], epi_copy(units[mu][1], units[mu][2])))
 
         for item in pending:
             epi_act(item[2], item[3], item[4])
         quantize(15, 3)
-        for g in range(4):
-            multiply(14, g)
-        for g in range(4):
-            multiply(15, g)
+        for mu in range(len(mm_done), 16):
+            for g in range(4):
+                if multiply(mu, g) and mu < 15:
+                    epi_act(units[mu][1], units[mu][2], epi_copy(units[mu][1], units[mu][2]))
         zs = epip.tile([P, 512], F32, name="zs", tag="zs")
         ga = epip.tile([P, 4, 128], F32, name="act1", tag="act1")
         ot = outp.tile([P, 4, 128], F32, name="ot", tag="ot")

@@ -33,6 +33,7 @@ H_STEP = 3
 ACT_LAG = 2
 TP_BUFS = 7
 ACC_BUFS = 1
+TPV_BUFS = 0
 VE_MOD = 16
 VE_PH = 2
 XFIRST = 0
@@ -41,14 +42,38 @@ BIAS_AFTER = 6
 BIAS_STEP = 7
 PC_LEAD = 2
 DVE_ORDER = 1
+ODD_PC = 2
+EVEN_PC = 2
+EVEN_Q3 = 1
+FINAL_SPLIT = 0
+BYG = 0
+LOAD_UNIT = 0
+RAW_UNITS = 4
+FIRST_PIECES = 1
+SPLIT_UNTIL = 1
+NPIECE = 4
+ZS_ACT = 0
+MULT_POOL = 0
+H_EV_DVE = 0
+NA_ODD = -1
+LAST_ALT = 0
+LAST_HALF = 0
 PC_POS = 0
 
 
+def na_of(s):
+    return NA_ODD if (NA_ODD >= 0 and s % 2 == 1) else NA
+
+
 def precopied(s, jj, g):
-    return FIRST_Q <= s < LAST_Q and 4 * jj + g < NA
+    if BYG:
+        return FIRST_Q <= s < LAST_Q and g >= 4 - BYG
+    return FIRST_Q <= s < LAST_Q and 4 * jj + g < na_of(s)
 
 
 def vector_copies(s, g):
+    if s == NSTEP - 1 and LAST_ALT:
+        return (LAST_ALT >> g) % 2 == 1
     return s >= FIRST_Q and (4 * s + g) % VE_MOD == VE_PH
 
 
@@ -65,7 +90,7 @@ def tile_naivelstm_pa_kernel(tc, x, h, w_ii, w_ig, w_hi, w_hg, b_ii, b_hi, b_ig,
 
     with ExitStack() as ctx:
         const = ctx.enter_context(tc.tile_pool(name="const", bufs=1))
-        rawp = ctx.enter_context(tc.tile_pool(name="rawp", bufs=RAW_BUFS))
+        rawp = ctx.enter_context(tc.tile_pool(name="rawp", bufs=RAW_UNITS if LOAD_UNIT else RAW_BUFS))
         rawdp = ctx.enter_context(tc.tile_pool(name="rawdp", bufs=4))
         grpp = ctx.enter_context(tc.tile_pool(name="grpp", bufs=8))
         codep = ctx.enter_context(tc.tile_pool(name="codep", bufs=CODE_BUFS))
@@ -73,6 +98,7 @@ def tile_naivelstm_pa_kernel(tc, x, h, w_ii, w_ig, w_hi, w_hg, b_ii, b_hi, b_ig,
         outp = ctx.enter_context(tc.tile_pool(name="outp", bufs=4))
         tpp = ctx.enter_context(tc.psum_pool(name="tpp", bufs=TP_BUFS))
         accp = ctx.enter_context(tc.psum_pool(name="accp", bufs=ACC_BUFS))
+        tpv = ctx.enter_context(tc.psum_pool(name="tpv", bufs=TPV_BUFS)) if TPV_BUFS else tpp
         ctx.enter_context(tc.manual_schedule())
 
         raw = {}
@@ -83,24 +109,58 @@ def tile_naivelstm_pa_kernel(tc, x, h, w_ii, w_ig, w_hi, w_hg, b_ii, b_hi, b_ig,
         acts = {}
         to_store = []
 
+        def load_unit(u_idx):
+            w, n, gate, from_x = units[u_idx]
+            t4 = rawp.tile([P, 4, K], BF16, name="raw", tag="raw")
+            src4 = w.rearrange("(p n j) k -> p n j k", n=4, j=4)[:, n, :, :]
+            raw[2 * u_idx] = t4[:, 0:2, :]
+            raw[2 * u_idx + 1] = t4[:, 2:4, :]
+            if u_idx == 0:
+                for g in range(4):
+                    nc.sync.dma_start(out=t4[:, 0:2, 512 * g : 512 * (g + 1)], in_=src4[:, 0:2, 512 * g : 512 * (g + 1)])
+                nc.sync.dma_start(out=t4[:, 2:4, :], in_=src4[:, 2:4, :])
+            elif u_idx == 15:
+                nc.sync.dma_start(out=t4[:, 0:2, :], in_=src4[:, 0:2, :])
+                nc.sync.dma_start(out=t4[:, 2:4, :], in_=src4[:, 2:4, :])
+            else:
+                nc.sync.dma_start(out=t4[:], in_=src4)
+
         def load(s):
             u_idx, jp = divmod(s, 2)
+            if LOAD_UNIT:
+                if jp == 0:
+                    load_unit(u_idx)
+                return
             w, n, gate, from_x = units[u_idx]
             t = rawp.tile([P, 2, K], BF16, name="raw", tag="raw")
             src = w.rearrange("(p n j) k -> p n j k", n=4, j=4)[:, n, 2 * jp : 2 * jp + 2, :]
-            if s == 0 or (LAST_PIECES and s == NSTEP - 1):
+            if (s == 0 and FIRST_PIECES == 4) or (LAST_PIECES and s == NSTEP - 1):
                 for g in range(4):
                     nc.sync.dma_start(out=t[:, :, 512 * g : 512 * (g + 1)], in_=src[:, :, 512 * g : 512 * (g + 1)])
+            elif s == 0 and FIRST_PIECES == 2:
+                for g in range(2):
+                    nc.sync.dma_start(out=t[:, :, 1024 * g : 1024 * (g + 1)], in_=src[:, :, 1024 * g : 1024 * (g + 1)])
+            elif 0 < s < SPLIT_UNTIL:
+                w_ = K // NPIECE
+                for g in range(NPIECE):
+                    nc.sync.dma_start(out=t[:, :, w_ * g : w_ * (g + 1)], in_=src[:, :, w_ * g : w_ * (g + 1)])
             else:
                 nc.sync.dma_start(out=t[:], in_=src)
-            raw[s] = t
+            raw[s] = t[:]
 
         def precopy(s):
             if FIRST_Q <= s < LAST_Q:
-                d = rawdp.tile([P, 2, NA, 128], F32, name="rawd", tag="rawd")
-                words = raw[s][:].rearrange("p j k -> p (j k)").bitcast(F32)
+                if BYG:
+                    d = rawdp.tile([P, 2, 2, BYG, 128], F32, name="rawd", tag="rawd")
+                    w4 = raw[s].bitcast(F32)[:, :, 256 * (4 - BYG) : 1024]
+                    nc.vector.tensor_copy(out=d[:], in_=w4.rearrange("p j (a m u) -> p u j a m", a=BYG, u=2))
+                    rawd[s] = d
+                    return
+                na = na_of(s)
+                d = rawdp.tile([P, 2, na, 128], F32, name="rawd", tag="rawd")
+                words = raw[s].rearrange("p j k -> p (j k)").bitcast(F32)
                 nc.vector.tensor_copy(
-                    out=d[:], in_=words[:, 0 : 256 * NA].rearrange("p (a m u) -> p u a m", a=NA, u=2)
+                    out=d[:], in_=words[:, 0 : 256 * na].rearrange("p (a m u) -> p u a m", a=na, u=2)
                 )
                 rawd[s] = d
 
@@ -116,6 +176,17 @@ def tile_naivelstm_pa_kernel(tc, x, h, w_ii, w_ig, w_hi, w_hg, b_ii, b_hi, b_ig,
             ws = codep.tile([P, 512], U8, name="ws", tag="ws", align_bytes=64)
             nc.vector.quantize_mx(out=wc[:].bitcast(E5), scales=ws[:], in_=grp[(u_idx, g)][:])
             codes[(u_idx, g)] = (wc, ws)
+
+        def quantize_half(u_idx, g, hf):
+            if hf == 0:
+                wc = codep.tile([P, 512], U32, name="wc", tag="wc", align_bytes=64)
+                ws = codep.tile([P, 512], U8, name="ws", tag="ws", align_bytes=64)
+                codes[(u_idx, g)] = (wc, ws)
+            wc, ws = codes[(u_idx, g)]
+            cs = slice(256 * hf, 256 * (hf + 1))
+            nc.vector.quantize_mx(
+                out=wc[:, cs].bitcast(E5), scales=ws[:, cs], in_=grp[(u_idx, g)][:, 1024 * hf : 1024 * (hf + 1)]
+            )
 
         def multiply(u_idx, g):
             w, n, gate, from_x = units[u_idx]
@@ -137,7 +208,10 @@ def tile_naivelstm_pa_kernel(tc, x, h, w_ii, w_ig, w_hi, w_hg, b_ii, b_hi, b_ig,
 
         def epi_copy(n, gate):
             zs = epip.tile([P, 512], F32, name="zs", tag="zs")
-            nc.vector.tensor_copy(out=zs[:], in_=acc[(n, gate)][:])
+            if (ZS_ACT >> gate) % 2 == 1:
+                nc.scalar.copy(out=zs[:], in_=acc[(n, gate)][:])
+            else:
+                nc.vector.tensor_copy(out=zs[:], in_=acc[(n, gate)][:])
             return zs
 
         def epi_act(n, gate, zs):
@@ -155,7 +229,9 @@ def tile_naivelstm_pa_kernel(tc, x, h, w_ii, w_ig, w_hi, w_hg, b_ii, b_hi, b_ig,
 
         def epi_store(n):
             ot = outp.tile([P, 4, 128], F32, name="ot", tag="ot")
-            nc.vector.tensor_tensor(out=ot[:], in0=acts[(n, 0)][:], in1=acts[(n, 1)][:], op=ALU.mult)
+            (nc.gpsimd if MULT_POOL else nc.vector).tensor_tensor(
+                out=ot[:], in0=acts[(n, 0)][:], in1=acts[(n, 1)][:], op=ALU.mult
+            )
             to_store.append((n, ot))
 
         def store_ready():
@@ -203,8 +279,12 @@ def tile_naivelstm_pa_kernel(tc, x, h, w_ii, w_ig, w_hi, w_hg, b_ii, b_hi, b_ig,
             u_idx, jp = divmod(s, 2)
             if s + LEAD < NSTEP:
                 load_more(s + LEAD)
-            if jp == 0 and u_idx > 0 and not DVE_ORDER:
+            if jp == 0 and u_idx > 0 and (not DVE_ORDER or EVEN_Q3 == 0):
                 quantize(u_idx - 1, 3)
+            if DVE_ORDER and jp == 0 and EVEN_PC == 0 and s + 2 < NSTEP:
+                precopy(s + 2)
+            if LAST_HALF and s == NSTEP - 1:
+                quantize_half(15, 3, 0)
             if s == X_STEP:
                 nc.vector.tensor_copy(
                     out=xgrp[:].rearrange("p (g b j) -> p g b j", g=4, j=4),
@@ -229,37 +309,49 @@ def tile_naivelstm_pa_kernel(tc, x, h, w_ii, w_ig, w_hi, w_hg, b_ii, b_hi, b_ig,
                                 bank[:, u, 128 * gg : 128 * (gg + 1)], hw[:, 256 * g + u : 256 * (g + 1) : 2], ident[:]
                             )
                     dst = hgrp[:].bitcast(F32)[:, 512 * gp : 512 * (gp + 1)].rearrange("p (c u) -> p c u", u=2)
-                    evacuate(False, dst, bank)
+                    evacuate(H_EV_DVE == 1, dst, bank)
                 nc.vector.quantize_mx(out=hc[:].bitcast(E4), scales=hs[:], in_=hgrp[:])
 
             for g in range(4):
                 if jp == 0:
                     grp[(u_idx, g)] = grpp.tile([P, 2048], BF16, name="grp", tag="grp", align_bytes=64)
-                bank = tpp.tile([P, 2, 256], F32, name="bank", tag="tp")
+                dst = grp[(u_idx, g)][:].bitcast(F32)[:, 512 * jp : 512 * (jp + 1)]
+                halves = LAST_HALF and s == NSTEP - 1 and g == 3
+                if not halves:
+                    bank = (tpv if vector_copies(s, g) else tpp).tile([P, 2, 256], F32, name="bank", tag="tp")
                 for jj in range(2):
+                    if halves:
+                        bank = tpp.tile([P, 2, 128], F32, name="half", tag="tp")
                     for u in range(2):
-                        if precopied(s, jj, g):
+                        if precopied(s, jj, g) and BYG:
+                            src = rawd[s][:, u, jj, g - (4 - BYG), :]
+                        elif precopied(s, jj, g):
                             src = rawd[s][:, u, 4 * jj + g, :]
                         else:
                             src = raw[s][:, jj, :].bitcast(F32)[:, 256 * g + u : 256 * (g + 1) : 2]
-                        nc.tensor.transpose(bank[:, u, 128 * jj : 128 * (jj + 1)], src, ident[:])
-                dst = grp[(u_idx, g)][:].bitcast(F32)[:, 512 * jp : 512 * (jp + 1)]
-                evacuate(vector_copies(s, g), dst.rearrange("p (c u) -> p c u", u=2), bank)
+                        c0 = 0 if halves else 128 * jj
+                        nc.tensor.transpose(bank[:, u, c0 : c0 + 128], src, ident[:])
+                    if halves:
+                        evacuate(jj == 1, dst[:, 256 * jj : 256 * (jj + 1)].rearrange("p (c u) -> p c u", u=2), bank)
+                if not halves:
+                    evacuate(vector_copies(s, g), dst.rearrange("p (c u) -> p c u", u=2), bank)
                 if jp == 1 and g >= 1 and not DVE_ORDER:
                     quantize(u_idx, g - 1)
                 if s + PC_LEAD < NSTEP and PC_POS == g + 1 and not DVE_ORDER:
                     precopy(s + PC_LEAD)
                 if DVE_ORDER:
-                    if jp == 1 and g in (1, 2):
-                        quantize(u_idx, g - 1)
-                    if jp == 1 and g == 3:
-                        if s + 2 < NSTEP:
+                    if jp == 1 and g >= 1:
+                        if ODD_PC == g - 1 and s + 2 < NSTEP:
                             precopy(s + 2)
-                        quantize(u_idx, 2)
+                        quantize(u_idx, g - 1)
+                        if ODD_PC == 3 and g == 3 and s + 2 < NSTEP:
+                            precopy(s + 2)
                     if jp == 0 and g == 2:
-                        if u_idx > 0:
+                        if EVEN_PC == 1 and s + 2 < NSTEP:
+                            precopy(s + 2)
+                        if u_idx > 0 and EVEN_Q3 == 1:
                             quantize(u_idx - 1, 3)
-                        if s + 2 < NSTEP:
+                        if EVEN_PC == 2 and s + 2 < NSTEP:
                             precopy(s + 2)
 
             still = []
@@ -286,7 +378,10 @@ def tile_naivelstm_pa_kernel(tc, x, h, w_ii, w_ig, w_hi, w_hg, b_ii, b_hi, b_ig,
 
         for item in pending:
             epi_act(item[2], item[3], item[4])
-        quantize(15, 3)
+        if LAST_HALF:
+            quantize_half(15, 3, 1)
+        else:
+            quantize(15, 3)
         for mu in range(len(mm_done), 16):
             for g in range(4):
                 if multiply(mu, g) and mu < 15:
@@ -304,4 +399,8 @@ def tile_naivelstm_pa_kernel(tc, x, h, w_ii, w_ig, w_hi, w_hg, b_ii, b_hi, b_ig,
             )
         for j in range(4):
             nc.vector.tensor_tensor(out=ot[:, j, :], in0=acts[(3, 0)][:, j, :], in1=ga[:, j, :], op=ALU.mult)
-        nc.sync.dma_start(out=out.rearrange("(p n j) b -> p n j b", n=4, j=4)[:, 3, :, :], in_=ot[:])
+            if FINAL_SPLIT and (j + 1) % FINAL_SPLIT == 0:
+                js = slice(j + 1 - FINAL_SPLIT, j + 1)
+                nc.sync.dma_start(out=out.rearrange("(p n j) b -> p n j b", n=4, j=4)[:, 3, js, :], in_=ot[:, js, :])
+        if not FINAL_SPLIT:
+            nc.sync.dma_start(out=out.rearrange("(p n j) b -> p n j b", n=4, j=4)[:, 3, :, :], in_=ot[:])

@@ -46,7 +46,7 @@ ODD_PC = 2
 EVEN_PC = 2
 EVEN_Q3 = 1
 FINAL_SPLIT = 0
-BYG = 0
+BYG = 2
 LOAD_UNIT = 0
 RAW_UNITS = 4
 FIRST_PIECES = 1

@@ -24,8 +24,8 @@ NA = 5
 FIRST_Q = 5
 LAST_Q = 32
 MMU = 1
-MM_LAG = 2
-CODE_BUFS = 12
+MM_LAG = 3
+CODE_BUFS = 16
 X_AFTER = 1
 X_STEP = 0
 H_AFTER = 2
@@ -46,6 +46,9 @@ ODD_PC = 2
 EVEN_PC = 2
 EVEN_Q3 = 1
 FINAL_SPLIT = 0
+ODD_LATE = 0
+LEAD1 = 0
+END_HALVES = 0
 BYG = 2
 LOAD_UNIT = 0
 RAW_UNITS = 4
@@ -270,7 +273,7 @@ def tile_naivelstm_pa_kernel(tc, x, h, w_ii, w_ig, w_hi, w_hg, b_ii, b_hi, b_ig,
         for s in range(LEAD):
             load_more(s)
 
-        for s in range(PC_LEAD):
+        for s in range(1 if LEAD1 else PC_LEAD):
             precopy(s)
         pending = []
         mm_done = []
@@ -283,7 +286,7 @@ def tile_naivelstm_pa_kernel(tc, x, h, w_ii, w_ig, w_hi, w_hg, b_ii, b_hi, b_ig,
                 quantize(u_idx - 1, 3)
             if DVE_ORDER and jp == 0 and EVEN_PC == 0 and s + 2 < NSTEP:
                 precopy(s + 2)
-            if LAST_HALF and s == NSTEP - 1:
+            if (LAST_HALF or END_HALVES) and s == NSTEP - 1:
                 quantize_half(15, 3, 0)
             if s == X_STEP:
                 nc.vector.tensor_copy(
@@ -340,19 +343,35 @@ def tile_naivelstm_pa_kernel(tc, x, h, w_ii, w_ig, w_hi, w_hg, b_ii, b_hi, b_ig,
                 if s + PC_LEAD < NSTEP and PC_POS == g + 1 and not DVE_ORDER:
                     precopy(s + PC_LEAD)
                 if DVE_ORDER:
+                    last_u = END_HALVES and u_idx == 15
                     if jp == 1 and g >= 1:
-                        if ODD_PC == g - 1 and s + 2 < NSTEP:
+                        if ODD_PC == g - 1 and s + 2 < NSTEP and not (END_HALVES and s + 2 == NSTEP - 1) and not LEAD1 and not ODD_LATE:
                             precopy(s + 2)
-                        quantize(u_idx, g - 1)
-                        if ODD_PC == 3 and g == 3 and s + 2 < NSTEP:
+                        if last_u:
+                            quantize_half(u_idx, g - 1, 1)
+                        else:
+                            quantize(u_idx, g - 1)
+                        if LEAD1 and g == 1 and s + 1 < NSTEP:
+                            precopy(s + 1)
+                        if ODD_PC == 3 and g == 3 and s + 2 < NSTEP and not LEAD1:
                             precopy(s + 2)
                     if jp == 0 and g == 2:
                         if EVEN_PC == 1 and s + 2 < NSTEP:
                             precopy(s + 2)
                         if u_idx > 0 and EVEN_Q3 == 1:
                             quantize(u_idx - 1, 3)
-                        if EVEN_PC == 2 and s + 2 < NSTEP:
+                        if ODD_LATE and s + 1 < NSTEP:
+                            precopy(s + 1)
+                        if EVEN_PC == 2 and s + 2 < NSTEP and not LEAD1:
                             precopy(s + 2)
+                        if LEAD1 and s + 1 < NSTEP:
+                            precopy(s + 1)
+                        if last_u:
+                            quantize_half(u_idx, 0, 0)
+                            precopy(s + 1)
+                            quantize_half(u_idx, 1, 0)
+                    if jp == 0 and g == 3 and last_u:
+                        quantize_half(u_idx, 2, 0)
 
             still = []
             for item in pending:
@@ -378,7 +397,7 @@ def tile_naivelstm_pa_kernel(tc, x, h, w_ii, w_ig, w_hi, w_hg, b_ii, b_hi, b_ig,
 
         for item in pending:
             epi_act(item[2], item[3], item[4])
-        if LAST_HALF:
+        if LAST_HALF or END_HALVES:
             quantize_half(15, 3, 1)
         else:
             quantize(15, 3)

from contextlib import ExitStack

import concourse.mybir as mybir
from concourse.masks import make_identity

F32 = mybir.dt.float32
BF16 = mybir.dt.bfloat16
U32 = mybir.dt.uint32
U8 = mybir.dt.uint8
E4 = mybir.dt.float8_e4m3fn_x4
E5 = mybir.dt.float8_e5m2_x4
ACT = mybir.ActivationFunctionType
ALU = mybir.AluOpType

P = 128
K = 2048
NSTEP = 32
RAW_BUFS = 8
LEAD = RAW_BUFS - 1

FLOPS = 2 * 4 * 2048 * 2048 * 128

NA = 5
FIRST_Q = 5
LAST_Q = 32
MMU = 1
MM_LAG = 3
CODE_BUFS = 16
X_AFTER = 1
X_STEP = 0
H_AFTER = 2
H_STEP = 3
ACT_LAG = 2
TP_BUFS = 7
ACC_BUFS = 1
TPV_BUFS = 0
VE_MOD = 16
VE_PH = 2
XFIRST = 0
LAST_PIECES = 0
BIAS_AFTER = 6
BIAS_STEP = 7
PC_LEAD = 2
DVE_ORDER = 1
ODD_PC = 2
EVEN_PC = 2
EVEN_Q3 = 1
FINAL_SPLIT = 0
ODD_LATE = 0
LEAD1 = 0
END_HALVES = 0
BYG = 2
LOAD_UNIT = 0
RAW_UNITS = 4
FIRST_PIECES = 1
SPLIT_UNTIL = 1
NPIECE = 4
ZS_ACT = 0
MULT_POOL = 0
H_EV_DVE = 0
NA_ODD = -1
LAST_ALT = 0
LAST_HALF = 0
PC_POS = 0


def na_of(s):
    return NA_ODD if (NA_ODD >= 0 and s % 2 == 1) else NA


def precopied(s, jj, g):
    if BYG:
        return FIRST_Q <= s < LAST_Q and g >= 4 - BYG
    return FIRST_Q <= s < LAST_Q and 4 * jj + g < na_of(s)


def vector_copies(s, g):
    if s == NSTEP - 1 and LAST_ALT:
        return (LAST_ALT >> g) % 2 == 1
    return s >= FIRST_Q and (4 * s + g) % VE_MOD == VE_PH


def tile_naivelstm_pa_kernel(tc, x, h, w_ii, w_ig, w_hi, w_hg, b_ii, b_hi, b_ig, b_hg, out):
    nc = tc.nc
    units = []
    for n in range(4):
        if n == 0 and XFIRST:
            order = ((w_ii, 0, True), (w_ig, 1, True), (w_hi, 0, False), (w_hg, 1, False))
        else:
            order = ((w_ii, 0, True), (w_hi, 0, False), (w_ig, 1, True), (w_hg, 1, False))
        for w, gate, from_x in order:
            units.append((w, n, gate, from_x))

    with ExitStack() as ctx:
        const = ctx.enter_context(tc.tile_pool(name="const", bufs=1))
        rawp = ctx.enter_context(tc.tile_pool(name="rawp", bufs=RAW_UNITS if LOAD_UNIT else RAW_BUFS))
        rawdp = ctx.enter_context(tc.tile_pool(name="rawdp", bufs=4))
        grpp = ctx.enter_context(tc.tile_pool(name="grpp", bufs=8))
        codep = ctx.enter_context(tc.tile_pool(name="codep", bufs=CODE_BUFS))
        epip = ctx.enter_context(tc.tile_pool(name="epip", bufs=2))
        outp = ctx.enter_context(tc.tile_pool(name="outp", bufs=4))
        tpp = ctx.enter_context(tc.psum_pool(name="tpp", bufs=TP_BUFS))
        accp = ctx.enter_context(tc.psum_pool(name="accp", bufs=ACC_BUFS))
        tpv = ctx.enter_context(tc.psum_pool(name="tpv", bufs=TPV_BUFS)) if TPV_BUFS else tpp
        ctx.enter_context(tc.manual_schedule())

        raw = {}
        rawd = {}
        grp = {}
        codes = {}
        acc = {}
        acts = {}
        to_store = []

        def load_unit(u_idx):
            w, n, gate, from_x = units[u_idx]
            t4 = rawp.tile([P, 4, K], BF16, name="raw", tag="raw")
            src4 = w.rearrange("(p n j) k -> p n j k", n=4, j=4)[:, n, :, :]
            raw[2 * u_idx] = t4[:, 0:2, :]
            raw[2 * u_idx + 1] = t4[:, 2:4, :]
            if u_idx == 0:
                for g in range(4):
                    nc.sync.dma_start(out=t4[:, 0:2, 512 * g : 512 * (g + 1)], in_=src4[:, 0:2, 512 * g : 512 * (g + 1)])
                nc.sync.dma_start(out=t4[:, 2:4, :], in_=src4[:, 2:4, :])
            elif u_idx == 15:
                nc.sync.dma_start(out=t4[:, 0:2, :], in_=src4[:, 0:2, :])
                nc.sync.dma_start(out=t4[:, 2:4, :], in_=src4[:, 2:4, :])
            else:
                nc.sync.dma_start(out=t4[:], in_=src4)

        def load(s):
            u_idx, jp = divmod(s, 2)
            if LOAD_UNIT:
                if jp == 0:
                    load_unit(u_idx)
                return
            w, n, gate, from_x = units[u_idx]
            t = rawp.tile([P, 2, K], BF16, name="raw", tag="raw")
            src = w.rearrange("(p n j) k -> p n j k", n=4, j=4)[:, n, 2 * jp : 2 * jp + 2, :]
            if (s == 0 and FIRST_PIECES == 4) or (LAST_PIECES and s == NSTEP - 1):
                for g in range(4):
                    nc.sync.dma_start(out=t[:, :, 512 * g : 512 * (g + 1)], in_=src[:, :, 512 * g : 512 * (g + 1)])
            elif s == 0 and FIRST_PIECES == 2:
                for g in range(2):
                    nc.sync.dma_start(out=t[:, :, 1024 * g : 1024 * (g + 1)], in_=src[:, :, 1024 * g : 1024 * (g + 1)])
            elif 0 < s < SPLIT_UNTIL:
                w_ = K // NPIECE
                for g in range(NPIECE):
                    nc.sync.dma_start(out=t[:, :, w_ * g : w_ * (g + 1)], in_=src[:, :, w_ * g : w_ * (g + 1)])
            else:
                nc.sync.dma_start(out=t[:], in_=src)
            raw[s] = t[:]

        def precopy(s):
            if FIRST_Q <= s < LAST_Q:
                if BYG:
                    d = rawdp.tile([P, 2, 2, BYG, 128], F32, name="rawd", tag="rawd")
                    w4 = raw[s].bitcast(F32)[:, :, 256 * (4 - BYG) : 1024]
                    nc.vector.tensor_copy(out=d[:], in_=w4.rearrange("p j (a m u) -> p u j a m", a=BYG, u=2))
                    rawd[s] = d
                    return
                na = na_of(s)
                d = rawdp.tile([P, 2, na, 128], F32, name="rawd", tag="rawd")
                words = raw[s].rearrange("p j k -> p (j k)").bitcast(F32)
                nc.vector.tensor_copy(
                    out=d[:], in_=words[:, 0 : 256 * na].rearrange("p (a m u) -> p u a m", a=na, u=2)
                )
                rawd[s] = d

        def evacuate(eng_is_vector, dst, bank):
            src = bank[:].rearrange("p u c -> p c u")
            if eng_is_vector:
                nc.vector.tensor_copy(out=dst, in_=src)
            else:
                nc.scalar.copy(out=dst, in_=src)

        def quantize(u_idx, g):
            wc = codep.tile([P, 512], U32, name="wc", tag="wc", align_bytes=64)
            ws = codep.tile([P, 512], U8, name="ws", tag="ws", align_bytes=64)
            nc.vector.quantize_mx(out=wc[:].bitcast(E5), scales=ws[:], in_=grp[(u_idx, g)][:])
            codes[(u_idx, g)] = (wc, ws)

        def quantize_half(u_idx, g, hf):
            if hf == 0:
                wc = codep.tile([P, 512], U32, name="wc", tag="wc", align_bytes=64)
                ws = codep.tile([P, 512], U8, name="ws", tag="ws", align_bytes=64)
                codes[(u_idx, g)] = (wc, ws)
            wc, ws = codes[(u_idx, g)]
            cs = slice(256 * hf, 256 * (hf + 1))
            nc.vector.quantize_mx(
                out=wc[:, cs].bitcast(E5), scales=ws[:, cs], in_=grp[(u_idx, g)][:, 1024 * hf : 1024 * (hf + 1)]
            )

        def multiply(u_idx, g):
            w, n, gate, from_x = units[u_idx]
            if from_x and g == 0:
                acc[(n, gate)] = accp.tile([P, 512], F32, name="acc", tag="acc")
            ac, asc = (xc, xs) if from_x else (hc, hs)
            wc, ws = codes[(u_idx, g)]
            cols = slice(128 * g, 128 * (g + 1))
            nc.tensor.matmul_mx(
                out=acc[(n, gate)][:],
                lhsT=ac[:, cols].bitcast(E4),
                lhsT_scale=asc[:, cols],
                rhs=wc[:].bitcast(E5),
                rhs_scale=ws[:],
                start=(from_x and g == 0),
                stop=(not from_x and g == 3),
            )
            return not from_x and g == 3

        def epi_copy(n, gate):
            zs = epip.tile([P, 512], F32, name="zs", tag="zs")
            if (ZS_ACT >> gate) % 2 == 1:
                nc.scalar.copy(out=zs[:], in_=acc[(n, gate)][:])
            else:
                nc.vector.tensor_copy(out=zs[:], in_=acc[(n, gate)][:])
            return zs

        def epi_act(n, gate, zs):
            zt = tpp.tile([P, 4, 128], F32, name="zt", tag="tp")
            for j in range(4):
                nc.tensor.transpose(zt[:, j, :], zs[:, 128 * j : 128 * (j + 1)], ident[:])
            a = epip.tile([P, 4, 128], F32, name="act%d" % gate, tag="act%d" % gate)
            func = ACT.Sigmoid if gate == 0 else ACT.Tanh
            for j in range(4):
                col = 4 * n + j
                nc.scalar.activation(
                    out=a[:, j, :], in_=zt[:, j, :], func=func, bias=bias[:, gate, col : col + 1], scale=1.0
                )
            acts[(n, gate)] = a

        def epi_store(n):
            ot = outp.tile([P, 4, 128], F32, name="ot", tag="ot")
            (nc.gpsimd if MULT_POOL else nc.vector).tensor_tensor(
                out=ot[:], in0=acts[(n, 0)][:], in1=acts[(n, 1)][:], op=ALU.mult
            )
            to_store.append((n, ot))

        def store_ready():
            for n, ot in to_store:
                nc.sync.dma_start(out=out.rearrange("(p n j) b -> p n j b", n=4, j=4)[:, n, :, :], in_=ot[:])
            to_store.clear()

        braw = const.tile([P, 4, 16], BF16, name="braw")
        warm = const.tile([P, 1], F32, name="warm")
        warm2 = const.tile([P, 1], F32, name="warm2")
        nc.vector.memset(warm[:], 0.0)
        nc.scalar.activation(out=warm2[:], in_=warm[:], func=ACT.Sigmoid)
        ident = const.tile([P, P], F32, name="ident")
        make_identity(nc, ident[:])

        xraw = const.tile([P, 4, 512], BF16, name="xraw")
        xgrp = const.tile([P, 2048], BF16, name="xgrp", align_bytes=64)
        xc = const.tile([P, 512], U32, name="xc", align_bytes=64)
        xs = const.tile([P, 512], U8, name="xs", align_bytes=64)
        hraw = const.tile([P, K], BF16, name="hraw")
        hgrp = const.tile([P, 2048], BF16, name="hgrp", align_bytes=64)
        hc = const.tile([P, 512], U32, name="hc", align_bytes=64)
        hs = const.tile([P, 512], U8, name="hs", align_bytes=64)
        bias = const.tile([P, 2, 16], F32, name="bias")

        def load_more(s):
            load(s)
            if s == X_AFTER:
                nc.sync.dma_start(out=xraw[:], in_=x.rearrange("(g p j) b -> p g (j b)", p=P, j=4))
            if s == H_AFTER:
                nc.sync.dma_start(out=hraw[:], in_=h)
            if s == BIAS_AFTER:
                for i, bvec in enumerate((b_ii, b_hi, b_ig, b_hg)):
                    nc.sync.dma_start(out=braw[:, i, :], in_=bvec.rearrange("(p c) o -> p (c o)", c=16))

        for s in range(LEAD):
            load_more(s)

        for s in range(1 if LEAD1 else PC_LEAD):
            precopy(s)
        pending = []
        mm_done = []

        for s in range(NSTEP):
            u_idx, jp = divmod(s, 2)
            if s + LEAD < NSTEP:
                load_more(s + LEAD)
            if jp == 0 and u_idx > 0 and (not DVE_ORDER or EVEN_Q3 == 0):
                quantize(u_idx - 1, 3)
            if DVE_ORDER and jp == 0 and EVEN_PC == 0 and s + 2 < NSTEP:
                precopy(s + 2)
            if (LAST_HALF or END_HALVES) and s == NSTEP - 1:
                quantize_half(15, 3, 0)
            if s == X_STEP:
                nc.vector.tensor_copy(
                    out=xgrp[:].rearrange("p (g b j) -> p g b j", g=4, j=4),
                    in_=xraw[:].rearrange("p g (j b) -> p g b j", j=4),
                )
                nc.vector.quantize_mx(out=xc[:].bitcast(E4), scales=xs[:], in_=xgrp[:])
            if s == BIAS_STEP:
                for gate in range(2):
                    nc.vector.tensor_tensor(
                        out=bias[:, gate, :], in0=braw[:, 2 * gate, :], in1=braw[:, 2 * gate + 1, :], op=ALU.add
                    )
            if s + PC_LEAD < NSTEP and PC_POS == 0 and not DVE_ORDER:
                precopy(s + PC_LEAD)
            if s == H_STEP:
                hw = hraw[:].bitcast(F32)
                for gp in range(2):
                    bank = tpp.tile([P, 2, 256], F32, name="hbank", tag="tp")
                    for gg in range(2):
                        g = 2 * gp + gg
                        for u in range(2):
                            nc.tensor.transpose(
                                bank[:, u, 128 * gg : 128 * (gg + 1)], hw[:, 256 * g + u : 256 * (g + 1) : 2], ident[:]
                            )
                    dst = hgrp[:].bitcast(F32)[:, 512 * gp : 512 * (gp + 1)].rearrange("p (c u) -> p c u", u=2)
                    evacuate(H_EV_DVE == 1, dst, bank)
                nc.vector.quantize_mx(out=hc[:].bitcast(E4), scales=hs[:], in_=hgrp[:])

            for g in range(4):
                if jp == 0:
                    grp[(u_idx, g)] = grpp.tile([P, 2048], BF16, name="grp", tag="grp", align_bytes=64)
                dst = grp[(u_idx, g)][:].bitcast(F32)[:, 512 * jp : 512 * (jp + 1)]
                halves = LAST_HALF and s == NSTEP - 1 and g == 3
                if not halves:
                    bank = (tpv if vector_copies(s, g) else tpp).tile([P, 2, 256], F32, name="bank", tag="tp")
                for jj in range(2):
                    if halves:
                        bank = tpp.tile([P, 2, 128], F32, name="half", tag="tp")
                    for u in range(2):
                        if precopied(s, jj, g) and BYG:
                            src = rawd[s][:, u, jj, g - (4 - BYG), :]
                        elif precopied(s, jj, g):
                            src = rawd[s][:, u, 4 * jj + g, :]
                        else:
                            src = raw[s][:, jj, :].bitcast(F32)[:, 256 * g + u : 256 * (g + 1) : 2]
                        c0 = 0 if halves else 128 * jj
                        nc.tensor.transpose(bank[:, u, c0 : c0 + 128], src, ident[:])
                    if halves:
                        evacuate(jj == 1, dst[:, 256 * jj : 256 * (jj + 1)].rearrange("p (c u) -> p c u", u=2), bank)
                if not halves:
                    evacuate(vector_copies(s, g), dst.rearrange("p (c u) -> p c u", u=2), bank)
                if jp == 1 and g >= 1 and not DVE_ORDER:
                    quantize(u_idx, g - 1)
                if s + PC_LEAD < NSTEP and PC_POS == g + 1 and not DVE_ORDER:
                    precopy(s + PC_LEAD)
                if DVE_ORDER:
                    last_u = END_HALVES and u_idx == 15
                    if jp == 1 and g >= 1:
                        if ODD_PC == g - 1 and s + 2 < NSTEP and not (END_HALVES and s + 2 == NSTEP - 1) and not LEAD1 and not ODD_LATE:
                            precopy(s + 2)
                        if last_u:
                            quantize_half(u_idx, g - 1, 1)
                        else:
                            quantize(u_idx, g - 1)
                        if LEAD1 and g == 1 and s + 1 < NSTEP:
                            precopy(s + 1)
                        if ODD_PC == 3 and g == 3 and s + 2 < NSTEP and not LEAD1:
                            precopy(s + 2)
                    if jp == 0 and g == 2:
                        if EVEN_PC == 1 and s + 2 < NSTEP:
                            precopy(s + 2)
                        if u_idx > 0 and EVEN_Q3 == 1:
                            quantize(u_idx - 1, 3)
                        if ODD_LATE and s + 1 < NSTEP:
                            precopy(s + 1)
                        if EVEN_PC == 2 and s + 2 < NSTEP and not LEAD1:
                            precopy(s + 2)
                        if LEAD1 and s + 1 < NSTEP:
                            precopy(s + 1)
                        if last_u:
                            quantize_half(u_idx, 0, 0)
                            precopy(s + 1)
                            quantize_half(u_idx, 1, 0)
                    if jp == 0 and g == 3 and last_u:
                        quantize_half(u_idx, 2, 0)

            still = []
            for item in pending:
                if item[0] > s:
                    still.append(item)
                elif item[1] == "act":
                    epi_act(item[2], item[3], item[4])
                    if item[3] == 1:
                        still.append((s + 1, "store", item[2]))
                else:
                    epi_store(item[2])
            pending = still
            if s + LEAD >= NSTEP - 1:
                store_ready()

            if (s - MM_LAG + 1) % (2 * MMU) == 0 and s > MM_LAG:
                q = (s - MM_LAG + 1) // (2 * MMU) - 1
                for mu in range(q * MMU, (q + 1) * MMU):
                    mm_done.append(mu)
                    for g in range(4):
                        if multiply(mu, g):
                            pending.append((s + ACT_LAG, "act", units[mu][1], units[mu][2], epi_copy(units[mu][1], units[mu][2])))

        for item in pending:
            epi_act(item[2], item[3], item[4])
        if LAST_HALF or END_HALVES:
            quantize_half(15, 3, 1)
        else:
            quantize(15, 3)
        for mu in range(len(mm_done), 16):
            for g in range(4):
                if multiply(mu, g) and mu < 15:
                    epi_act(units[mu][1], units[mu][2], epi_copy(units[mu][1], units[mu][2]))
        zs = epip.tile([P, 512], F32, name="zs", tag="zs")
        ga = epip.tile([P, 4, 128], F32, name="act1", tag="act1")
        ot = outp.tile([P, 4, 128], F32, name="ot", tag="ot")
        for j in range(4):
            nc.vector.tensor_copy(out=zs[:, 128 * j : 128 * (j + 1)], in_=acc[(3, 1)][:, 128 * j : 128 * (j + 1)])
        for j in range(4):
            zt = tpp.tile([P, 4, 128], F32, name="zt", tag="tp")
            nc.tensor.transpose(zt[:, 0, :], zs[:, 128 * j : 128 * (j + 1)], ident[:])
            nc.scalar.activation(
                out=ga[:, j, :], in_=zt[:, 0, :], func=ACT.Tanh, bias=bias[:, 1, 12 + j : 13 + j], scale=1.0
            )
        for j in range(4):
            nc.vector.tensor_tensor(out=ot[:, j, :], in0=acts[(3, 0)][:, j, :], in1=ga[:, j, :], op=ALU.mult)
            if FINAL_SPLIT and (j + 1) % FINAL_SPLIT == 0:
                js = slice(j + 1 - FINAL_SPLIT, j + 1)
                nc.sync.dma_start(out=out.rearrange("(p n j) b -> p n j b", n=4, j=4)[:, 3, js, :], in_=ot[:, js, :])
        if not FINAL_SPLIT:
            nc.sync.dma_start(out=out.rearrange("(p n j) b -> p n j b", n=4, j=4)[:, 3, :, :], in_=ot[:])
